import numpy as np
import ml_dtypes


def mxq(x, axis, fmt="e4m3"):
    dtype, down = {"e4m3": (ml_dtypes.float8_e4m3fn, 7), "e5m2": (ml_dtypes.float8_e5m2, 14)}[fmt]
    v = np.moveaxis(np.asarray(x, np.float32).astype(ml_dtypes.bfloat16).astype(np.float64), axis, -1)
    blocks = v.reshape(v.shape[:-1] + (-1, 32))
    amax = np.abs(blocks).max(-1, keepdims=True)
    byte = np.maximum(np.where(amax > 0, np.frexp(amax)[1] - 1 + 127, 0) - down, 1)
    scale = np.exp2(byte - 127.0)
    codes = (blocks / scale).astype(np.float32).astype(dtype).astype(np.float64)
    return np.moveaxis((codes * scale).reshape(v.shape), -1, axis)


WIDE = False


def mx_kscale(k):
    if not WIDE:
        return np.ones(k)
    levels = np.array([18, -18])
    if k % 512:
        return np.exp2(np.random.permutation(np.resize(levels, k // 32))).repeat(32)
    a = np.empty((k // 512, 16))
    for p in range(k // 512):
        a[p, :8] = np.random.permutation(np.resize(levels, 8))
        for g in range(8):
            far = levels[np.abs(levels - a[p, g]) >= 10]
            a[p, g + 8] = far[np.random.randint(len(far))]
    return np.exp2(a.ravel()).repeat(32)


BF16 = ml_dtypes.bfloat16


def bf(x):
    return np.asarray(x, np.float32).astype(BF16)


def f64(x):
    return np.asarray(x).astype(np.float64)


B, SQ, SK, D, DV = 4, 1024, 1024, 128, 512


def setup_inputs():
    s = mx_kscale(SQ)[:, None]
    u = mx_kscale(DV)
    v = mx_kscale(SK)[:, None]
    qk = bf(1.0 + 0.1 * np.random.standard_normal((1, 1)))
    qk_scaling_factor = bf(1.5 + 0.1 * np.random.standard_normal((1, 1)))
    query0 = bf(np.random.standard_normal((B, SQ, D)))
    key0 = bf(np.random.standard_normal((B, SK, D)))
    value0 = bf(np.random.standard_normal((B, SK, DV)) * 1.5 / np.sqrt(SK))
    g = bf(np.random.standard_normal((B, SQ, DV)) * np.exp2(np.random.randint(-6, 1, (B, SQ, 1))) * 4.0 / s * u)
    score_divisor = np.sqrt(D) * f64(qk_scaling_factor)
    return {"qk": qk,
            "qk_scaling_factor": qk_scaling_factor,
            "query": bf(f64(query0) * s),
            "key": bf(f64(key0) / v),
            "value": bf(f64(value0) * v / u),
            "score_divisor": np.asarray(score_divisor, np.float32),
            "grad_out": g}


def reference(qk, qk_scaling_factor, query, key, value, score_divisor, grad_out):
    gq = mxq(f64(grad_out), 2, "e5m2")
    vq = mxq(f64(value), 2, "e4m3")
    dp = gq @ vq.transpose(0, 2, 1)
    ds = dp / f64(score_divisor)
    dquery = mxq(ds, 2, "e5m2") @ mxq(f64(key), 1, "e4m3")
    dkey = mxq(ds, 1, "e5m2").transpose(0, 2, 1) @ mxq(f64(query), 1, "e4m3")
    return dquery, dkey

@@ -1,0 +1,291 @@
+from contextlib import ExitStack
+
+import concourse.mybir as mybir
+from concourse.masks import make_identity
+
+F32 = mybir.dt.float32
+BF16 = mybir.dt.bfloat16
+U32 = mybir.dt.uint32
+U8 = mybir.dt.uint8
+E4M3X4 = mybir.dt.float8_e4m3fn_x4
+E5M2X4 = mybir.dt.float8_e5m2_x4
+COPY = mybir.ActivationFunctionType.Copy
+
+B, SQ, SK, D, DV = 4, 1024, 1024, 128, 512
+P = 128
+FLOPS = 2 * B * SQ * SK * (DV + 2 * D)
+BYTES = 2 * B * (SQ + SK) * (DV + D) + 4 * B * (SQ + SK) * D + 4
+
+STEPS = 4 * B
+
+
+def tile_model_v_kernel(
+    tc, qk, qk_scaling_factor, query, key, value, score_divisor, grad_out, out_0, out_1
+):
+    nc = tc.nc
+    with ExitStack() as ctx:
+        const = ctx.enter_context(tc.tile_pool(name="const", bufs=1))
+        raw = ctx.enter_context(tc.tile_pool(name="raw", bufs=1))
+        work = ctx.enter_context(tc.tile_pool(name="work", bufs=3))
+        ring = ctx.enter_context(tc.psum_pool(name="ring", bufs=6))
+        accp = ctx.enter_context(tc.psum_pool(name="accp", bufs=1))
+        ctx.enter_context(tc.manual_schedule())
+
+        ident = const.tile([P, P], F32, name="ident")
+        make_identity(nc, ident[:])
+        div = const.tile([P, 1], F32, name="div")
+        nc.scalar.dma_start(
+            out=div[:], in_=score_divisor.rearrange("a b -> (a b)").partition_broadcast(P)
+        )
+        recip = const.tile([P, 1], F32, name="recip")
+        warm = const.tile([P, 1], F32, name="warm")
+
+        pieces = {}
+        kq_raw = {}
+
+        def gv_view(m):
+            b, r = divmod(m, 4)
+            if r % 2 == 0:
+                c = r // 2
+                return value[b, 512 * c : 512 * (c + 1), :].rearrange("(h r e) v -> r h e v", h=2, e=2)
+            g = r // 2
+            return grad_out[b, 512 * g : 512 * (g + 1), :].rearrange("(p h e) v -> p h e v", h=2, e=2)
+
+        for b in range(B):
+            for m in range(4 * b, 4 * b + 4):
+                view = gv_view(m)
+                if m < 2:
+                    for h in range(2):
+                        t = raw.tile([P, 2, DV], BF16, name="raw%d_%d" % (m, h), tag="raw%d_%d" % (m, h))
+                        nc.sync.dma_start(out=t[:], in_=view[:, h])
+                        pieces[(m, h)] = t[:]
+                else:
+                    t = raw.tile([P, 2, 2, DV], BF16, name="raw%d" % m, tag="raw%d" % m)
+                    nc.sync.dma_start(out=t[:], in_=view)
+                    for h in range(2):
+                        pieces[(m, h)] = t[:, h]
+            for which, src in ((0, key), (1, query)):
+                t = raw.tile([P, 2, 4, D], BF16, name="kq%d_%d" % (b, which), tag="kq%d_%d" % (b, which))
+                nc.sync.dma_start(out=t[:], in_=src[b].rearrange("(c p j) d -> p c j d", c=2, j=4))
+                for c in range(2):
+                    kq_raw[4 * b + 2 * which + c] = t[:, c]
+
+        grp = {}
+        gvc = {}
+        kqg = {}
+        kqc = {}
+        dsx = {}
+        gqx = {}
+        gtx = {}
+        qqc = {}
+        qtc = {}
+        bank = {}
+        acc = {}
+        ot = {}
+        otp = {}
+
+        def transpose_gv(m, h):
+            words = pieces[(m, h)].bitcast(F32)
+            t = ring.tile([P, 4, P], F32, name="gvp", tag="ring")
+            for s in range(2):
+                for u in range(2):
+                    nc.tensor.transpose(t[:, 2 * s + u, :], words[:, s, u::2], ident[:])
+            bank[("gv", m, h)] = t
+
+        def copy_gv(m, h, eng):
+            if h == 0:
+                grp[m] = work.tile([P, 512, 4], BF16, name="grp", tag="grp", align_bytes=64)
+            flat = grp[m][:].rearrange("p c t -> p (c t)").bitcast(F32)
+            t = bank[("gv", m, h)][:]
+            if m % 2 == 0:
+                dst = flat.rearrange("p (u h r f) -> p h u r f", u=2, h=2, f=4)[:, h]
+                src = t.rearrange("p f (r u) -> p u r f", u=2)
+            else:
+                dst = flat.rearrange("p (h s q u) -> p h s q u", h=2, s=2, u=2)[:, h]
+                src = t.rearrange("p (s u) q -> p s q u", u=2)
+            eng(out=dst, in_=src)
+
+        def quant(src, kind, tag, bufs, width):
+            codes = work.tile([P, width], U32, name=tag + "c", tag=tag + "c", bufs=bufs, align_bytes=64)
+            scales = work.tile([P, width], U8, name=tag + "s", tag=tag + "s", bufs=bufs, align_bytes=64)
+            nc.vector.quantize_mx(
+                out=codes[:].bitcast(kind),
+                scales=scales[:],
+                in_=src[:].rearrange("p c t -> p (c t)"),
+            )
+            return codes, scales
+
+        def quant_gv(m):
+            gvc[m] = quant(grp[m], E4M3X4 if m % 2 == 0 else E5M2X4, "gv", 6, 512)
+
+        def inter_kq(k):
+            kqg[k] = work.tile([P, D, 4], BF16, name="kqg", tag="kqg", bufs=2, align_bytes=64)
+            nc.vector.tensor_copy(
+                out=kqg[k][:].rearrange("p (c i) t -> p c t i", i=4),
+                in_=kq_raw[k].rearrange("p t (c i) -> p c t i", i=4),
+            )
+
+        def quant_kq(k):
+            kqc[k] = quant(kqg[k], E4M3X4, "kq", 12, D)
+
+        def mm_dp(n, t):
+            b, r = divmod(n, 4)
+            g, c = divmod(r, 2)
+            vc, vs = gvc[4 * b + 2 * c]
+            gc, gs = gvc[4 * b + 2 * g + 1]
+            o = ring.tile([P, 512], F32, name="dpb", tag="ring")
+            cols = slice(P * t, P * (t + 1))
+            nc.tensor.matmul_mx(
+                out=o[:],
+                lhsT=gc[:, cols].bitcast(E5M2X4),
+                lhsT_scale=gs[:, cols],
+                rhs=vc[:].bitcast(E4M3X4),
+                rhs_scale=vs[:],
+                start=True,
+                stop=True,
+            )
+            bank[("dp", n, t)] = o
+
+        def copy_dp(n, t):
+            if t == 0:
+                dsx[n] = work.tile([P, 4, 512], BF16, name="ds", tag="ds", align_bytes=64)
+            nc.scalar.activation(
+                out=dsx[n][:, t, :], in_=bank[("dp", n, t)][:], func=COPY, scale=recip[:, 0:1]
+            )
+
+        def transpose_ds(n, h):
+            words = dsx[n][:].bitcast(F32)
+            t = ring.tile([P, 4, P], F32, name="dst", tag="ring")
+            for s in range(2):
+                for u in range(2):
+                    nc.tensor.transpose(t[:, 2 * s + u, :], words[:, 2 * h + s, P * u : P * (u + 1)], ident[:])
+            bank[("ds", n, h)] = t
+
+        def copy_dst(n, h):
+            if h == 0:
+                gtx[n] = work.tile([P, 512, 4], BF16, name="gt", tag="gt", align_bytes=64)
+            flat = gtx[n][:].rearrange("p c t -> p (c t)").bitcast(F32)
+            nc.scalar.copy(
+                out=flat.rearrange("p (h s q u) -> p h s q u", h=2, s=2, u=2)[:, h],
+                in_=bank[("ds", n, h)][:].rearrange("p (s u) q -> p s q u", u=2),
+            )
+
+        def inter_ds(n):
+            gqx[n] = work.tile([P, 512, 4], BF16, name="gq", tag="gq", align_bytes=64)
+            nc.vector.tensor_copy(
+                out=gqx[n][:].rearrange("p (c i) t -> p c t i", i=4),
+                in_=dsx[n][:].rearrange("p t (c i) -> p c t i", i=4),
+            )
+
+        def quant_q(n):
+            qqc[n] = quant(gqx[n], E5M2X4, "qq", 6, 512)
+
+        def quant_t(n):
+            qtc[n] = quant(gtx[n], E5M2X4, "qt", 6, 512)
+
+        def mm_out(o, i):
+            which, b, x = o
+            if i == 0:
+                acc[o] = accp.tile([P, 512], F32, name="acc", tag="acc")
+            sc, ss = kqc[4 * b + 2 * which + i]
+            mc, ms = qtc[4 * b + 2 * x + i] if which == 0 else qqc[4 * b + 2 * i + x]
+            nc.tensor.matmul_mx(
+                out=acc[o][:],
+                lhsT=sc[:].bitcast(E4M3X4),
+                lhsT_scale=ss[:],
+                rhs=mc[:].bitcast(E5M2X4),
+                rhs_scale=ms[:],
+                start=(i == 0),
+                stop=(i == 1),
+            )
+
+        def copy_acc(o, eng):
+            which, b, x = o
+            ot[o] = work.tile([P, 4, P], F32, name="ot", tag="ot", bufs=2)
+            src = acc[o][:]
+            if which == 0:
+                eng(out=ot[o][:], in_=src.rearrange("p (t q) -> p t q", t=4))
+            else:
+                eng(
+                    out=ot[o][:].rearrange("p (u e) q -> p u e q", u=2),
+                    in_=src.rearrange("p (u q e) -> p u e q", u=2, e=2),
+                )
+
+        def transpose_out(o):
+            which, b, x = o
+            otp[o] = accp.tile([P, 4, P], F32, name="otp", tag="otp")
+            for t in range(4):
+                nc.tensor.transpose(otp[o][:, t, :], ot[o][:, t, :], ident[:])
+
+        def store_out(o, eng):
+            which, b, x = o
+            rows = work.tile([P, 4, D], F32, name="rows", tag="rows")
+            eng(out=rows[:], in_=otp[o][:])
+            dst = out_0 if which == 0 else out_1
+            nc.sync.dma_start(
+                out=dst[b, 512 * x : 512 * (x + 1), :].rearrange("(p t) d -> p t d", t=4), in_=rows[:]
+            )
+
+        out_at = {}
+        for b in range(B):
+            out_at[4 * b + 4] = (0, b, 0)
+            out_at[4 * b + 5] = (1, b, 0)
+            out_at[4 * b + 6] = (1, b, 1)
+            out_at[4 * b + 7] = (0, b, 1)
+
+        sc = nc.scalar.copy
+        vc = nc.vector.tensor_copy
+
+        nc.vector.memset(warm[:], 1.0)
+        nc.scalar.activation(out=warm[:], in_=warm[:], func=COPY, scale=1.0)
+        for m in range(3):
+            for h in range(2):
+                transpose_gv(m, h)
+                copy_gv(m, h, sc if h == 0 else vc)
+            if m == 0:
+                nc.vector.reciprocal(out=recip[:], in_=div[:])
+            if m >= 1:
+                quant_gv(m - 1)
+
+        for n in range(STEPS + 5):
+            o = out_at.get(n)
+            po = out_at.get(n - 1)
+            dp = n < STEPS
+            dt = 1 <= n <= STEPS
+            gv = n + 3 < STEPS
+            for h in range(2):
+                if dp:
+                    mm_dp(n, 2 * h)
+                    mm_dp(n, 2 * h + 1)
+                if o:
+                    mm_out(o, h)
+                if dt:
+                    transpose_ds(n - 1, h)
+                if gv:
+                    transpose_gv(n + 3, h)
+                if h == 0 and po:
+                    transpose_out(po)
+                if dp:
+                    copy_dp(n, 2 * h)
+                    copy_dp(n, 2 * h + 1)
+                if dt:
+                    copy_dst(n - 1, h)
+                if gv:
+                    copy_gv(n + 3, h, sc)
+                if h == 0:
+                    if dt:
+                        inter_ds(n - 1)
+                    if 2 <= n <= STEPS + 1:
+                        quant_t(n - 2)
+                    if dt:
+                        quant_q(n - 1)
+                    if dp:
+                        inter_kq(n)
+                    if po:
+                        store_out(po, vc)
+                    if n + 2 < STEPS:
+                        quant_gv(n + 2)
+                    if dp:
+                        quant_kq(n)
+            if o:
+                copy_acc(o, vc)

@@ -10,6 +10,7 @@ U8 = mybir.dt.uint8
 E4M3X4 = mybir.dt.float8_e4m3fn_x4
 E5M2X4 = mybir.dt.float8_e5m2_x4
 COPY = mybir.ActivationFunctionType.Copy
+MULT = mybir.AluOpType.mult
 
 B, SQ, SK, D, DV = 4, 1024, 1024, 128, 512
 P = 128
@@ -17,6 +18,7 @@ FLOPS = 2 * B * SQ * SK * (DV + 2 * D)
 BYTES = 2 * B * (SQ + SK) * (DV + D) + 4 * B * (SQ + SK) * D + 4
 
 STEPS = 4 * B
+SCALAR_BIAS = 0.0
 
 
 def tile_model_v_kernel(
@@ -45,11 +47,10 @@ def tile_model_v_kernel(
 
         def gv_view(m):
             b, r = divmod(m, 4)
+            x = r // 2
             if r % 2 == 0:
-                c = r // 2
-                return value[b, 512 * c : 512 * (c + 1), :].rearrange("(h r e) v -> r h e v", h=2, e=2)
-            g = r // 2
-            return grad_out[b, 512 * g : 512 * (g + 1), :].rearrange("(p h e) v -> p h e v", h=2, e=2)
+                return value[b, 512 * x : 512 * (x + 1), :].rearrange("(h r e) v -> r h e v", h=2, e=2)
+            return grad_out[b, 512 * x : 512 * (x + 1), :].rearrange("(p h e) v -> p h e v", h=2, e=2)
 
         for b in range(B):
             for m in range(4 * b, 4 * b + 4):
@@ -67,8 +68,20 @@ def tile_model_v_kernel(
             for which, src in ((0, key), (1, query)):
                 t = raw.tile([P, 2, 4, D], BF16, name="kq%d_%d" % (b, which), tag="kq%d_%d" % (b, which))
                 nc.sync.dma_start(out=t[:], in_=src[b].rearrange("(c p j) d -> p c j d", c=2, j=4))
-                for c in range(2):
-                    kq_raw[4 * b + 2 * which + c] = t[:, c]
+                kq_raw[(which, b)] = t
+
+        load = {"s": SCALAR_BIAS, "v": 0.0}
+
+        def busy(eng, ns):
+            load[eng] += ns
+
+        def psum_copy(dst, src, eng=None):
+            if eng == "s" or (eng is None and load["s"] <= load["v"]):
+                busy("s", 445)
+                nc.scalar.copy(out=dst, in_=src)
+            else:
+                busy("v", 457)
+                nc.vector.tensor_copy(out=dst, in_=src)
 
         grp = {}
         gvc = {}
@@ -84,51 +97,59 @@ def tile_model_v_kernel(
         ot = {}
         otp = {}
 
-        def transpose_gv(m, h):
+        def gv_unit(m, h):
             words = pieces[(m, h)].bitcast(F32)
             t = ring.tile([P, 4, P], F32, name="gvp", tag="ring")
             for s in range(2):
                 for u in range(2):
                     nc.tensor.transpose(t[:, 2 * s + u, :], words[:, s, u::2], ident[:])
-            bank[("gv", m, h)] = t
-
-        def copy_gv(m, h, eng):
             if h == 0:
                 grp[m] = work.tile([P, 512, 4], BF16, name="grp", tag="grp", align_bytes=64)
             flat = grp[m][:].rearrange("p c t -> p (c t)").bitcast(F32)
-            t = bank[("gv", m, h)][:]
             if m % 2 == 0:
                 dst = flat.rearrange("p (u h r f) -> p h u r f", u=2, h=2, f=4)[:, h]
-                src = t.rearrange("p f (r u) -> p u r f", u=2)
+                src = t[:].rearrange("p f (r u) -> p u r f", u=2)
             else:
                 dst = flat.rearrange("p (h s q u) -> p h s q u", h=2, s=2, u=2)[:, h]
-                src = t.rearrange("p (s u) q -> p s q u", u=2)
-            eng(out=dst, in_=src)
+                src = t[:].rearrange("p (s u) q -> p s q u", u=2)
+            psum_copy(dst, src)
 
-        def quant(src, kind, tag, bufs, width):
-            codes = work.tile([P, width], U32, name=tag + "c", tag=tag + "c", bufs=bufs, align_bytes=64)
-            scales = work.tile([P, width], U8, name=tag + "s", tag=tag + "s", bufs=bufs, align_bytes=64)
-            nc.vector.quantize_mx(
-                out=codes[:].bitcast(kind),
-                scales=scales[:],
-                in_=src[:].rearrange("p c t -> p (c t)"),
-            )
+        def quant_tiles(tag, bufs):
+            codes = work.tile([P, 512], U32, name=tag + "c", tag=tag + "c", bufs=bufs, align_bytes=64)
+            scales = work.tile([P, 512], U8, name=tag + "s", tag=tag + "s", bufs=bufs, align_bytes=64)
             return codes, scales
 
-        def quant_gv(m):
-            gvc[m] = quant(grp[m], E4M3X4 if m % 2 == 0 else E5M2X4, "gv", 6, 512)
-
-        def inter_kq(k):
-            kqg[k] = work.tile([P, D, 4], BF16, name="kqg", tag="kqg", bufs=2, align_bytes=64)
-            nc.vector.tensor_copy(
-                out=kqg[k][:].rearrange("p (c i) t -> p c t i", i=4),
-                in_=kq_raw[k].rearrange("p t (c i) -> p c t i", i=4),
+        def quant(src, kind, pair, lo=0, hi=512):
+            codes, scales = pair
+            busy("v", 30 + 0.2235 * 4 * (hi - lo))
+            nc.vector.quantize_mx(
+                out=codes[:, lo:hi].bitcast(kind),
+                scales=scales[:, lo:hi],
+                in_=src[:, lo:hi, :].rearrange("p c t -> p (c t)"),
             )
 
-        def quant_kq(k):
-            kqc[k] = quant(kqg[k], E4M3X4, "kq", 12, D)
+        def quant_gv(m):
+            gvc[m] = quant_tiles("gv", 6)
+            quant(grp[m], E4M3X4 if m % 2 == 0 else E5M2X4, gvc[m])
 
-        def mm_dp(n, t):
+        def inter_kq(which, b):
+            t = work.tile([P, 2, D, 4], BF16, name="kqg", tag="kqg", bufs=2, align_bytes=64)
+            kqg[(which, b)] = t
+            busy("v", 30 + 522)
+            nc.vector.tensor_copy(out=t[:], in_=kq_raw[(which, b)][:].rearrange("p c j d -> p c d j"))
+
+        def quant_kq(which, b):
+            codes = work.tile([P, 2, D], U32, name="kqc", tag="kqc", bufs=4, align_bytes=64)
+            scales = work.tile([P, 2, D], U8, name="kqs", tag="kqs", bufs=4, align_bytes=64)
+            busy("v", 30 + 229)
+            nc.vector.quantize_mx(
+                out=codes[:].rearrange("p c d -> p (c d)").bitcast(E4M3X4),
+                scales=scales[:].rearrange("p c d -> p (c d)"),
+                in_=kqg[(which, b)][:].rearrange("p c d j -> p (c d j)"),
+            )
+            kqc[(which, b)] = (codes, scales)
+
+        def dp_unit(n, t):
             b, r = divmod(n, 4)
             g, c = divmod(r, 2)
             vc, vs = gvc[4 * b + 2 * c]
@@ -144,148 +165,180 @@ def tile_model_v_kernel(
                 start=True,
                 stop=True,
             )
-            bank[("dp", n, t)] = o
-
-        def copy_dp(n, t):
             if t == 0:
                 dsx[n] = work.tile([P, 4, 512], BF16, name="ds", tag="ds", align_bytes=64)
-            nc.scalar.activation(
-                out=dsx[n][:, t, :], in_=bank[("dp", n, t)][:], func=COPY, scale=recip[:, 0:1]
-            )
+            if load["s"] <= load["v"]:
+                busy("s", 455)
+                nc.scalar.activation(out=dsx[n][:, t, :], in_=o[:], func=COPY, scale=recip[:, 0:1])
+            else:
+                busy("v", 467)
+                nc.vector.tensor_scalar(
+                    out=dsx[n][:, t, :], in0=o[:], scalar1=recip[:, 0:1], scalar2=None, op0=MULT
+                )
 
-        def transpose_ds(n, h):
+        def dst_unit(n, h):
             words = dsx[n][:].bitcast(F32)
             t = ring.tile([P, 4, P], F32, name="dst", tag="ring")
             for s in range(2):
                 for u in range(2):
                     nc.tensor.transpose(t[:, 2 * s + u, :], words[:, 2 * h + s, P * u : P * (u + 1)], ident[:])
-            bank[("ds", n, h)] = t
-
-        def copy_dst(n, h):
             if h == 0:
                 gtx[n] = work.tile([P, 512, 4], BF16, name="gt", tag="gt", align_bytes=64)
             flat = gtx[n][:].rearrange("p c t -> p (c t)").bitcast(F32)
-            nc.scalar.copy(
-                out=flat.rearrange("p (h s q u) -> p h s q u", h=2, s=2, u=2)[:, h],
-                in_=bank[("ds", n, h)][:].rearrange("p (s u) q -> p s q u", u=2),
+            psum_copy(
+                flat.rearrange("p (h s q u) -> p h s q u", h=2, s=2, u=2)[:, h],
+                t[:].rearrange("p (s u) q -> p s q u", u=2),
             )
 
         def inter_ds(n):
             gqx[n] = work.tile([P, 512, 4], BF16, name="gq", tag="gq", align_bytes=64)
+            busy("v", 1062)
             nc.vector.tensor_copy(
                 out=gqx[n][:].rearrange("p (c i) t -> p c t i", i=4),
                 in_=dsx[n][:].rearrange("p t (c i) -> p c t i", i=4),
             )
 
         def quant_q(n):
-            qqc[n] = quant(gqx[n], E5M2X4, "qq", 6, 512)
+            qqc[n] = quant_tiles("qq", 6)
+            quant(gqx[n], E5M2X4, qqc[n])
 
         def quant_t(n):
-            qtc[n] = quant(gtx[n], E5M2X4, "qt", 6, 512)
+            qtc[n] = quant_tiles("qt", 6)
+            quant(gtx[n], E5M2X4, qtc[n])
 
-        def mm_out(o, i):
+        def mm_out(o, i, late):
             which, b, x = o
             if i == 0:
-                acc[o] = accp.tile([P, 512], F32, name="acc", tag="acc")
-            sc, ss = kqc[4 * b + 2 * which + i]
+                if late:
+                    acc[o] = ring.tile([P, 512], F32, name="accl", tag="ring")
+                else:
+                    acc[o] = accp.tile([P, 512], F32, name="acc", tag="acc")
+            sc, ss = kqc[(which, b)]
             mc, ms = qtc[4 * b + 2 * x + i] if which == 0 else qqc[4 * b + 2 * i + x]
             nc.tensor.matmul_mx(
                 out=acc[o][:],
-                lhsT=sc[:].bitcast(E4M3X4),
-                lhsT_scale=ss[:],
+                lhsT=sc[:, i, :].bitcast(E4M3X4),
+                lhsT_scale=ss[:, i, :],
                 rhs=mc[:].bitcast(E5M2X4),
                 rhs_scale=ms[:],
                 start=(i == 0),
                 stop=(i == 1),
             )
 
-        def copy_acc(o, eng):
+        def out_rows(o):
             which, b, x = o
-            ot[o] = work.tile([P, 4, P], F32, name="ot", tag="ot", bufs=2)
+            return (out_1 if which else out_0)[b, 512 * x : 512 * (x + 1), :]
+
+        def out_copy(o, eng=None):
+            which, b, x = o
+            ot[o] = work.tile([P, 4, P], F32, name="ot", tag="ot", bufs=3)
             src = acc[o][:]
             if which == 0:
-                eng(out=ot[o][:], in_=src.rearrange("p (t q) -> p t q", t=4))
+                psum_copy(ot[o][:], src.rearrange("p (t q) -> p t q", t=4), eng)
             else:
-                eng(
-                    out=ot[o][:].rearrange("p (u e) q -> p u e q", u=2),
-                    in_=src.rearrange("p (u q e) -> p u e q", u=2, e=2),
+                psum_copy(
+                    ot[o][:].rearrange("p (u e) q -> p u e q", u=2),
+                    src.rearrange("p (u q e) -> p u e q", u=2, e=2),
+                    eng,
                 )
 
-        def transpose_out(o):
-            which, b, x = o
-            otp[o] = accp.tile([P, 4, P], F32, name="otp", tag="otp")
+        def out_turn(o, late):
+            if late:
+                otp[o] = ring.tile([P, 4, P], F32, name="otpl", tag="ring")
+            else:
+                otp[o] = accp.tile([P, 4, P], F32, name="otp", tag="otp")
             for t in range(4):
                 nc.tensor.transpose(otp[o][:, t, :], ot[o][:, t, :], ident[:])
 
-        def store_out(o, eng):
-            which, b, x = o
-            rows = work.tile([P, 4, D], F32, name="rows", tag="rows")
-            eng(out=rows[:], in_=otp[o][:])
-            dst = out_0 if which == 0 else out_1
-            nc.sync.dma_start(
-                out=dst[b, 512 * x : 512 * (x + 1), :].rearrange("(p t) d -> p t d", t=4), in_=rows[:]
-            )
+        def out_store(o, eng=None):
+            rows = work.tile([P, 4, D], F32, name="rows", tag="rows", bufs=5)
+            psum_copy(rows[:], otp[o][:], eng)
+            nc.sync.dma_start(out=out_rows(o).rearrange("(p t) d -> p t d", t=4), in_=rows[:])
 
-        out_at = {}
-        for b in range(B):
-            out_at[4 * b + 4] = (0, b, 0)
-            out_at[4 * b + 5] = (1, b, 0)
-            out_at[4 * b + 6] = (1, b, 1)
-            out_at[4 * b + 7] = (0, b, 1)
-
-        sc = nc.scalar.copy
-        vc = nc.vector.tensor_copy
 
         nc.vector.memset(warm[:], 1.0)
         nc.scalar.activation(out=warm[:], in_=warm[:], func=COPY, scale=1.0)
-        for m in range(3):
-            for h in range(2):
-                transpose_gv(m, h)
-                copy_gv(m, h, sc if h == 0 else vc)
-            if m == 0:
-                nc.vector.reciprocal(out=recip[:], in_=div[:])
-            if m >= 1:
-                quant_gv(m - 1)
+        gv_unit(0, 0)
+        gv_unit(0, 1)
+        gv_unit(1, 0)
+        nc.vector.reciprocal(out=recip[:], in_=div[:])
+        quant_gv(0)
+        gvc[1] = quant_tiles("gv", 6)
+        quant(grp[1], E5M2X4, gvc[1], 0, 256)
+        gv_unit(1, 1)
 
-        for n in range(STEPS + 5):
+        out_at = {}
+        for b in range(B):
+            out_at[4 * b + 3] = (0, b, 0)
+            out_at[4 * b + 4] = (1, b, 0)
+            out_at[4 * b + 5] = (1, b, 1)
+            out_at[4 * b + 6] = (0, b, 1)
+
+        for n in range(STEPS):
             o = out_at.get(n)
             po = out_at.get(n - 1)
-            dp = n < STEPS
-            dt = 1 <= n <= STEPS
-            gv = n + 3 < STEPS
-            for h in range(2):
-                if dp:
-                    mm_dp(n, 2 * h)
-                    mm_dp(n, 2 * h + 1)
-                if o:
-                    mm_out(o, h)
-                if dt:
-                    transpose_ds(n - 1, h)
-                if gv:
-                    transpose_gv(n + 3, h)
-                if h == 0 and po:
-                    transpose_out(po)
-                if dp:
-                    copy_dp(n, 2 * h)
-                    copy_dp(n, 2 * h + 1)
-                if dt:
-                    copy_dst(n - 1, h)
-                if gv:
-                    copy_gv(n + 3, h, sc)
-                if h == 0:
-                    if dt:
-                        inter_ds(n - 1)
-                    if 2 <= n <= STEPS + 1:
-                        quant_t(n - 2)
-                    if dt:
-                        quant_q(n - 1)
-                    if dp:
-                        inter_kq(n)
-                    if po:
-                        store_out(po, vc)
-                    if n + 2 < STEPS:
-                        quant_gv(n + 2)
-                    if dp:
-                        quant_kq(n)
+            b = n // 4
+            ahead = n + 3 if n + 3 < STEPS else 0
+            if n:
+                inter_ds(n - 1)
+            if n % 4 in (2, 3):
+                quant_kq(n % 4 - 2, b)
+            dp_unit(n, 0)
+            dp_unit(n, 1)
             if o:
-                copy_acc(o, vc)
+                mm_out(o, 0, False)
+            if n >= 2:
+                quant_t(n - 2)
+            if n:
+                dst_unit(n - 1, 0)
+            else:
+                quant(grp[1], E5M2X4, gvc[1], 256, 512)
+                gv_unit(2, 0)
+                gv_unit(2, 1)
+            if po:
+                out_turn(po, False)
+            if ahead:
+                gv_unit(ahead, 0)
+            if n:
+                quant_q(n - 1)
+            if po:
+                out_store(po)
+            dp_unit(n, 2)
+            dp_unit(n, 3)
+            if o:
+                mm_out(o, 1, False)
+                out_copy(o)
+            if n + 2 < STEPS:
+                quant_gv(n + 2)
+            if n % 4 in (1, 2):
+                inter_kq(n % 4 - 1, b)
+            if n:
+                dst_unit(n - 1, 1)
+            if ahead:
+                gv_unit(ahead, 1)
+
+        n = STEPS
+        o0, o1, o2, o3 = (0, B - 1, 0), (1, B - 1, 0), (0, B - 1, 1), (1, B - 1, 1)
+        dst_unit(n - 1, 0)
+        quant_t(n - 2)
+        mm_out(o1, 0, True)
+        mm_out(o1, 1, True)
+        inter_ds(n - 1)
+        dst_unit(n - 1, 1)
+        out_turn(o0, False)
+        out_copy(o1)
+        out_store(o0)
+        out_turn(o1, True)
+        mm_out(o2, 0, True)
+        mm_out(o3, 0, True)
+        quant_t(n - 1)
+        mm_out(o2, 1, True)
+        out_store(o1)
+        quant_q(n - 1)
+        mm_out(o3, 1, True)
+        out_copy(o2, "s")
+        out_turn(o2, True)
+        out_copy(o3, "v")
+        out_turn(o3, True)
+        out_store(o2, "s")
+        out_store(o3, "v")

@@ -55,7 +55,7 @@ def tile_model_v_kernel(
         for b in range(B):
             for m in range(4 * b, 4 * b + 4):
                 view = gv_view(m)
-                if m < 2:
+                if m < 4:
                     for h in range(2):
                         t = raw.tile([P, 2, DV], BF16, name="raw%d_%d" % (m, h), tag="raw%d_%d" % (m, h))
                         nc.sync.dma_start(out=t[:], in_=view[:, h])
@@ -104,7 +104,7 @@ def tile_model_v_kernel(
                 for u in range(2):
                     nc.tensor.transpose(t[:, 2 * s + u, :], words[:, s, u::2], ident[:])
             if h == 0:
-                grp[m] = work.tile([P, 512, 4], BF16, name="grp", tag="grp", align_bytes=64)
+                grp[m] = work.tile([P, 512, 4], BF16, name="grp", tag="grp", bufs=4, align_bytes=64)
             flat = grp[m][:].rearrange("p c t -> p (c t)").bitcast(F32)
             if m % 2 == 0:
                 dst = flat.rearrange("p (u h r f) -> p h u r f", u=2, h=2, f=4)[:, h]
@@ -129,7 +129,7 @@ def tile_model_v_kernel(
             )
 
         def quant_gv(m):
-            gvc[m] = quant_tiles("gv", 6)
+            gvc[m] = quant_tiles("gv", 7)
             quant(grp[m], E4M3X4 if m % 2 == 0 else E5M2X4, gvc[m])
 
         def inter_kq(which, b):
@@ -186,8 +186,7 @@ def tile_model_v_kernel(
                 gtx[n] = work.tile([P, 512, 4], BF16, name="gt", tag="gt", align_bytes=64)
             flat = gtx[n][:].rearrange("p c t -> p (c t)").bitcast(F32)
             psum_copy(
-                flat.rearrange("p (h s q u) -> p h s q u", h=2, s=2, u=2)[:, h],
-                t[:].rearrange("p (s u) q -> p s q u", u=2),
+                flat.rearrange("p (q h f) -> p h q f", h=2, f=4)[:, h], t[:].rearrange("p f q -> p q f")
             )
 
         def inter_ds(n):
@@ -234,7 +233,7 @@ def tile_model_v_kernel(
             ot[o] = work.tile([P, 4, P], F32, name="ot", tag="ot", bufs=3)
             src = acc[o][:]
             if which == 0:
-                psum_copy(ot[o][:], src.rearrange("p (t q) -> p t q", t=4), eng)
+                psum_copy(ot[o][:], src.rearrange("p (q t) -> p t q", t=4), eng)
             else:
                 psum_copy(
                     ot[o][:].rearrange("p (u e) q -> p u e q", u=2),
@@ -256,16 +255,37 @@ def tile_model_v_kernel(
             nc.sync.dma_start(out=out_rows(o).rearrange("(p t) d -> p t d", t=4), in_=rows[:])
 
 
+        def out_blocks(o):
+            rows = work.tile([P, 16, 32], F32, name="blocks", tag="blocks", bufs=2, align_bytes=64)
+            busy("v", 457)
+            nc.vector.transpose(out=rows[:].rearrange("p b j -> p (b j)"), in_=acc[o][:])
+            for a in range(4):
+                lanes = slice(32 * a, 32 * (a + 1))
+                nc.sync.dma_start(
+                    out=out_rows(o)[:, lanes].rearrange("(b i) j -> i b j", i=32), in_=rows[lanes, :, :]
+                )
+
         nc.vector.memset(warm[:], 1.0)
         nc.scalar.activation(out=warm[:], in_=warm[:], func=COPY, scale=1.0)
         gv_unit(0, 0)
         gv_unit(0, 1)
-        gv_unit(1, 0)
         nc.vector.reciprocal(out=recip[:], in_=div[:])
+        gv_unit(1, 0)
         quant_gv(0)
-        gvc[1] = quant_tiles("gv", 6)
+        gvc[1] = quant_tiles("gv", 7)
         quant(grp[1], E5M2X4, gvc[1], 0, 256)
         gv_unit(1, 1)
+        quant(grp[1], E5M2X4, gvc[1], 256, 512)
+        gv_unit(2, 0)
+        dp_unit(0, 0)
+        dp_unit(0, 1)
+        gv_unit(2, 1)
+        dp_unit(0, 2)
+        dp_unit(0, 3)
+        quant_gv(2)
+        inter_ds(0)
+        gv_unit(3, 0)
+        gv_unit(3, 1)
 
         out_at = {}
         for b in range(B):
@@ -274,71 +294,71 @@ def tile_model_v_kernel(
             out_at[4 * b + 5] = (1, b, 1)
             out_at[4 * b + 6] = (0, b, 1)
 
-        for n in range(STEPS):
+        def blocked(o):
+            return o[0] == 0 and o[1] < B - 1
+
+        for n in range(1, STEPS):
             o = out_at.get(n)
             po = out_at.get(n - 1)
+            if po and blocked(po):
+                po = None
             b = n // 4
-            ahead = n + 3 if n + 3 < STEPS else 0
-            if n:
-                inter_ds(n - 1)
-            if n % 4 in (2, 3):
-                quant_kq(n % 4 - 2, b)
+            if n >= 2:
+                quant_t(n - 2)
             dp_unit(n, 0)
             dp_unit(n, 1)
             if o:
                 mm_out(o, 0, False)
-            if n >= 2:
-                quant_t(n - 2)
-            if n:
-                dst_unit(n - 1, 0)
-            else:
-                quant(grp[1], E5M2X4, gvc[1], 256, 512)
-                gv_unit(2, 0)
-                gv_unit(2, 1)
+            if n > 1:
+                inter_ds(n - 1)
+            dst_unit(n - 1, 0)
+            if n + 2 < STEPS:
+                quant_gv(n + 2)
             if po:
                 out_turn(po, False)
-            if ahead:
-                gv_unit(ahead, 0)
-            if n:
-                quant_q(n - 1)
-            if po:
-                out_store(po)
+            if n % 4 in (2, 3):
+                quant_kq(n % 4 - 2, b)
+            if n + 3 < STEPS:
+                gv_unit(n + 3, 0)
+            quant_q(n - 1)
             dp_unit(n, 2)
             dp_unit(n, 3)
             if o:
                 mm_out(o, 1, False)
-                out_copy(o)
-            if n + 2 < STEPS:
-                quant_gv(n + 2)
+                if blocked(o):
+                    out_blocks(o)
+                else:
+                    out_copy(o)
+            dst_unit(n - 1, 1)
+            if po:
+                out_store(po)
+            if n + 3 < STEPS:
+                gv_unit(n + 3, 1)
             if n % 4 in (1, 2):
                 inter_kq(n % 4 - 1, b)
-            if n:
-                dst_unit(n - 1, 1)
-            if ahead:
-                gv_unit(ahead, 1)
 
         n = STEPS
         o0, o1, o2, o3 = (0, B - 1, 0), (1, B - 1, 0), (0, B - 1, 1), (1, B - 1, 1)
+        inter_ds(n - 1)
         dst_unit(n - 1, 0)
-        quant_t(n - 2)
         mm_out(o1, 0, True)
         mm_out(o1, 1, True)
-        inter_ds(n - 1)
+        quant_t(n - 2)
         dst_unit(n - 1, 1)
         out_turn(o0, False)
-        out_copy(o1)
-        out_store(o0)
-        out_turn(o1, True)
+        out_copy(o1, "s")
+        out_store(o0, "s")
+        quant_t(n - 1)
         mm_out(o2, 0, True)
         mm_out(o3, 0, True)
-        quant_t(n - 1)
         mm_out(o2, 1, True)
-        out_store(o1)
         quant_q(n - 1)
         mm_out(o3, 1, True)
         out_copy(o2, "s")
-        out_turn(o2, True)
         out_copy(o3, "v")
+        out_turn(o1, True)
+        out_turn(o2, True)
         out_turn(o3, True)
+        out_store(o1, "v")
         out_store(o2, "s")
         out_store(o3, "v")

@@ -18,7 +18,7 @@ FLOPS = 2 * B * SQ * SK * (DV + 2 * D)
 BYTES = 2 * B * (SQ + SK) * (DV + D) + 4 * B * (SQ + SK) * D + 4
 
 STEPS = 4 * B
-SCALAR_BIAS = 0.0
+SCALAR_BIAS = -400.0
 
 
 def tile_model_v_kernel(
@@ -30,7 +30,7 @@ def tile_model_v_kernel(
         raw = ctx.enter_context(tc.tile_pool(name="raw", bufs=1))
         work = ctx.enter_context(tc.tile_pool(name="work", bufs=3))
         ring = ctx.enter_context(tc.psum_pool(name="ring", bufs=6))
-        accp = ctx.enter_context(tc.psum_pool(name="accp", bufs=1))
+        accp = ctx.enter_context(tc.psum_pool(name="accp", bufs=2))
         ctx.enter_context(tc.manual_schedule())
 
         ident = const.tile([P, P], F32, name="ident")
@@ -95,7 +95,6 @@ def tile_model_v_kernel(
         bank = {}
         acc = {}
         ot = {}
-        otp = {}
 
         def gv_unit(m, h):
             words = pieces[(m, h)].bitcast(F32)
@@ -119,7 +118,7 @@ def tile_model_v_kernel(
             scales = work.tile([P, 512], U8, name=tag + "s", tag=tag + "s", bufs=bufs, align_bytes=64)
             return codes, scales
 
-        def quant(src, kind, pair, lo=0, hi=512):
+        def quant(src, kind, pair, lo, hi):
             codes, scales = pair
             busy("v", 30 + 0.2235 * 4 * (hi - lo))
             nc.vector.quantize_mx(
@@ -130,7 +129,15 @@ def tile_model_v_kernel(
 
         def quant_gv(m):
             gvc[m] = quant_tiles("gv", 7)
-            quant(grp[m], E4M3X4 if m % 2 == 0 else E5M2X4, gvc[m])
+            quant(grp[m], E4M3X4 if m % 2 == 0 else E5M2X4, gvc[m], 0, 512)
+
+        def quant_q(n):
+            qqc[n] = quant_tiles("qq", 6)
+            quant(gqx[n], E5M2X4, qqc[n], 0, 512)
+
+        def quant_t(n):
+            qtc[n] = quant_tiles("qt", 6)
+            quant(gtx[n], E5M2X4, qtc[n], 0, 512)
 
         def inter_kq(which, b):
             t = work.tile([P, 2, D, 4], BF16, name="kqg", tag="kqg", bufs=2, align_bytes=64)
@@ -139,8 +146,8 @@ def tile_model_v_kernel(
             nc.vector.tensor_copy(out=t[:], in_=kq_raw[(which, b)][:].rearrange("p c j d -> p c d j"))
 
         def quant_kq(which, b):
-            codes = work.tile([P, 2, D], U32, name="kqc", tag="kqc", bufs=4, align_bytes=64)
-            scales = work.tile([P, 2, D], U8, name="kqs", tag="kqs", bufs=4, align_bytes=64)
+            codes = work.tile([P, 2, D], U32, name="kqc", tag="kqc", bufs=5, align_bytes=64)
+            scales = work.tile([P, 2, D], U8, name="kqs", tag="kqs", bufs=5, align_bytes=64)
             busy("v", 30 + 229)
             nc.vector.quantize_mx(
                 out=codes[:].rearrange("p c d -> p (c d)").bitcast(E4M3X4),
@@ -168,7 +175,7 @@ def tile_model_v_kernel(
             if t == 0:
                 dsx[n] = work.tile([P, 4, 512], BF16, name="ds", tag="ds", align_bytes=64)
             if load["s"] <= load["v"]:
-                busy("s", 455)
+                busy("s", 500)
                 nc.scalar.activation(out=dsx[n][:, t, :], in_=o[:], func=COPY, scale=recip[:, 0:1])
             else:
                 busy("v", 467)
@@ -191,25 +198,18 @@ def tile_model_v_kernel(
 
         def inter_ds(n):
             gqx[n] = work.tile([P, 512, 4], BF16, name="gq", tag="gq", align_bytes=64)
-            busy("v", 1062)
-            nc.vector.tensor_copy(
-                out=gqx[n][:].rearrange("p (c i) t -> p c t i", i=4),
-                in_=dsx[n][:].rearrange("p t (c i) -> p c t i", i=4),
-            )
-
-        def quant_q(n):
-            qqc[n] = quant_tiles("qq", 6)
-            quant(gqx[n], E5M2X4, qqc[n])
-
-        def quant_t(n):
-            qtc[n] = quant_tiles("qt", 6)
-            quant(gtx[n], E5M2X4, qtc[n])
+            for u in range(2):
+                busy("v", 531)
+                nc.vector.tensor_copy(
+                    out=gqx[n][:].rearrange("p (q u e) t -> p u q t e", u=2, e=2)[:, u],
+                    in_=dsx[n][:].rearrange("p t (u q e) -> p u q t e", u=2, e=2)[:, u],
+                )
 
         def mm_out(o, i, late):
             which, b, x = o
             if i == 0:
                 if late:
-                    acc[o] = ring.tile([P, 512], F32, name="accl", tag="ring")
+                    acc[o] = ring.tile([P, 512], F32, name="late", tag="ring")
                 else:
                     acc[o] = accp.tile([P, 512], F32, name="acc", tag="acc")
             sc, ss = kqc[(which, b)]
@@ -230,30 +230,20 @@ def tile_model_v_kernel(
 
         def out_copy(o, eng=None):
             which, b, x = o
-            ot[o] = work.tile([P, 4, P], F32, name="ot", tag="ot", bufs=3)
+            ot[o] = work.tile([P, 4, P], F32, name="ot", tag="ot", bufs=4)
             src = acc[o][:]
-            if which == 0:
-                psum_copy(ot[o][:], src.rearrange("p (q t) -> p t q", t=4), eng)
-            else:
-                psum_copy(
-                    ot[o][:].rearrange("p (u e) q -> p u e q", u=2),
-                    src.rearrange("p (u q e) -> p u e q", u=2, e=2),
-                    eng,
-                )
+            psum_copy(ot[o][:], src.rearrange("p (q t) -> p t q", t=4), eng)
 
-        def out_turn(o, late):
-            if late:
-                otp[o] = ring.tile([P, 4, P], F32, name="otpl", tag="ring")
-            else:
-                otp[o] = accp.tile([P, 4, P], F32, name="otp", tag="otp")
-            for t in range(4):
-                nc.tensor.transpose(otp[o][:, t, :], ot[o][:, t, :], ident[:])
+        def out_turn(o):
+            t = ring.tile([P, 4, P], F32, name="turn", tag="ring")
+            for j in range(4):
+                nc.tensor.transpose(t[:, j, :], ot[o][:, j, :], ident[:])
+            bank[o] = t
 
         def out_store(o, eng=None):
-            rows = work.tile([P, 4, D], F32, name="rows", tag="rows", bufs=5)
-            psum_copy(rows[:], otp[o][:], eng)
+            rows = work.tile([P, 4, D], F32, name="rows", tag="rows", bufs=4)
+            psum_copy(rows[:], bank[o][:], eng)
             nc.sync.dma_start(out=out_rows(o).rearrange("(p t) d -> p t d", t=4), in_=rows[:])
-
 
         def out_blocks(o):
             rows = work.tile([P, 16, 32], F32, name="blocks", tag="blocks", bufs=2, align_bytes=64)
@@ -265,8 +255,17 @@ def tile_model_v_kernel(
                     out=out_rows(o)[:, lanes].rearrange("(b i) j -> i b j", i=32), in_=rows[lanes, :, :]
                 )
 
+        zeros = const.tile([P, 512], BF16, name="zeros")
+        nc.gpsimd.memset(zeros[:], 0.0)
+
+        def keep_clock(times):
+            spin = accp.tile([P, 512], F32, name="acc", tag="acc")
+            for i in range(times):
+                nc.tensor.matmul(out=spin[:], lhsT=zeros[:, :P], rhs=zeros[:], start=True, stop=True)
+
         nc.vector.memset(warm[:], 1.0)
         nc.scalar.activation(out=warm[:], in_=warm[:], func=COPY, scale=1.0)
+        keep_clock(7)
         gv_unit(0, 0)
         gv_unit(0, 1)
         nc.vector.reciprocal(out=recip[:], in_=div[:])
@@ -294,16 +293,14 @@ def tile_model_v_kernel(
             out_at[4 * b + 5] = (1, b, 1)
             out_at[4 * b + 6] = (0, b, 1)
 
-        def blocked(o):
-            return o[0] == 0 and o[1] < B - 1
+        kq_at = {1: (0, 0), 2: (1, 0)}
+        for b in range(1, B):
+            kq_at[4 * b - 1] = (0, b)
+            kq_at[4 * b] = (1, b)
 
         for n in range(1, STEPS):
             o = out_at.get(n)
-            po = out_at.get(n - 1)
-            if po and blocked(po):
-                po = None
-            b = n // 4
-            if n >= 2:
+            if n > 1:
                 quant_t(n - 2)
             dp_unit(n, 0)
             dp_unit(n, 1)
@@ -314,10 +311,9 @@ def tile_model_v_kernel(
             dst_unit(n - 1, 0)
             if n + 2 < STEPS:
                 quant_gv(n + 2)
-            if po:
-                out_turn(po, False)
-            if n % 4 in (2, 3):
-                quant_kq(n % 4 - 2, b)
+            if n - 1 in kq_at:
+                which, kb = kq_at[n - 1]
+                quant_kq(which, kb)
             if n + 3 < STEPS:
                 gv_unit(n + 3, 0)
             quant_q(n - 1)
@@ -325,40 +321,42 @@ def tile_model_v_kernel(
             dp_unit(n, 3)
             if o:
                 mm_out(o, 1, False)
-                if blocked(o):
+                if n < STEPS - 1:
                     out_blocks(o)
                 else:
                     out_copy(o)
             dst_unit(n - 1, 1)
-            if po:
-                out_store(po)
             if n + 3 < STEPS:
                 gv_unit(n + 3, 1)
-            if n % 4 in (1, 2):
-                inter_kq(n % 4 - 1, b)
+            if n in kq_at:
+                which, kb = kq_at[n]
+                inter_kq(which, kb)
 
         n = STEPS
         o0, o1, o2, o3 = (0, B - 1, 0), (1, B - 1, 0), (0, B - 1, 1), (1, B - 1, 1)
         inter_ds(n - 1)
         dst_unit(n - 1, 0)
+        dst_unit(n - 1, 1)
         mm_out(o1, 0, True)
         mm_out(o1, 1, True)
         quant_t(n - 2)
-        dst_unit(n - 1, 1)
-        out_turn(o0, False)
+        out_turn(o0)
+        keep_clock(2)
         out_copy(o1, "s")
         out_store(o0, "s")
         quant_t(n - 1)
         mm_out(o2, 0, True)
         mm_out(o3, 0, True)
+        keep_clock(1)
         mm_out(o2, 1, True)
         quant_q(n - 1)
         mm_out(o3, 1, True)
+        keep_clock(1)
         out_copy(o2, "s")
         out_copy(o3, "v")
-        out_turn(o1, True)
-        out_turn(o2, True)
-        out_turn(o3, True)
+        out_turn(o1)
+        out_turn(o2)
+        out_turn(o3)
         out_store(o1, "v")
         out_store(o2, "s")
         out_store(o3, "v")

from contextlib import ExitStack

import concourse.mybir as mybir
from concourse.masks import make_identity

F32 = mybir.dt.float32
BF16 = mybir.dt.bfloat16
U32 = mybir.dt.uint32
U8 = mybir.dt.uint8
E4M3X4 = mybir.dt.float8_e4m3fn_x4
E5M2X4 = mybir.dt.float8_e5m2_x4
COPY = mybir.ActivationFunctionType.Copy
MULT = mybir.AluOpType.mult

B, SQ, SK, D, DV = 4, 1024, 1024, 128, 512
P = 128
FLOPS = 2 * B * SQ * SK * (DV + 2 * D)
BYTES = 2 * B * (SQ + SK) * (DV + D) + 4 * B * (SQ + SK) * D + 4

STEPS = 4 * B
SCALAR_BIAS = -400.0


def tile_model_v_kernel(
    tc, qk, qk_scaling_factor, query, key, value, score_divisor, grad_out, out_0, out_1
):
    nc = tc.nc
    with ExitStack() as ctx:
        const = ctx.enter_context(tc.tile_pool(name="const", bufs=1))
        raw = ctx.enter_context(tc.tile_pool(name="raw", bufs=1))
        work = ctx.enter_context(tc.tile_pool(name="work", bufs=3))
        ring = ctx.enter_context(tc.psum_pool(name="ring", bufs=6))
        accp = ctx.enter_context(tc.psum_pool(name="accp", bufs=2))
        ctx.enter_context(tc.manual_schedule())

        ident = const.tile([P, P], F32, name="ident")
        make_identity(nc, ident[:])
        div = const.tile([P, 1], F32, name="div")
        nc.scalar.dma_start(
            out=div[:], in_=score_divisor.rearrange("a b -> (a b)").partition_broadcast(P)
        )
        recip = const.tile([P, 1], F32, name="recip")
        warm = const.tile([P, 1], F32, name="warm")

        pieces = {}
        kq_raw = {}

        def gv_view(m):
            b, r = divmod(m, 4)
            x = r // 2
            if r % 2 == 0:
                return value[b, 512 * x : 512 * (x + 1), :].rearrange("(h r e) v -> r h e v", h=2, e=2)
            return grad_out[b, 512 * x : 512 * (x + 1), :].rearrange("(p h e) v -> p h e v", h=2, e=2)

        for b in range(B):
            for m in range(4 * b, 4 * b + 4):
                view = gv_view(m)
                if m < 4:
                    for h in range(2):
                        t = raw.tile([P, 2, DV], BF16, name="raw%d_%d" % (m, h), tag="raw%d_%d" % (m, h))
                        nc.sync.dma_start(out=t[:], in_=view[:, h])
                        pieces[(m, h)] = t[:]
                else:
                    t = raw.tile([P, 2, 2, DV], BF16, name="raw%d" % m, tag="raw%d" % m)
                    nc.sync.dma_start(out=t[:], in_=view)
                    for h in range(2):
                        pieces[(m, h)] = t[:, h]
            for which, src in ((0, key), (1, query)):
                t = raw.tile([P, 2, 4, D], BF16, name="kq%d_%d" % (b, which), tag="kq%d_%d" % (b, which))
                nc.sync.dma_start(out=t[:], in_=src[b].rearrange("(c p j) d -> p c j d", c=2, j=4))
                kq_raw[(which, b)] = t

        load = {"s": SCALAR_BIAS, "v": 0.0}

        def busy(eng, ns):
            load[eng] += ns

        def psum_copy(dst, src, eng=None):
            if eng == "s" or (eng is None and load["s"] <= load["v"]):
                busy("s", 445)
                nc.scalar.copy(out=dst, in_=src)
            else:
                busy("v", 457)
                nc.vector.tensor_copy(out=dst, in_=src)

        grp = {}
        gvc = {}
        kqg = {}
        kqc = {}
        dsx = {}
        gqx = {}
        gtx = {}
        qqc = {}
        qtc = {}
        bank = {}
        acc = {}
        ot = {}

        def gv_unit(m, h):
            words = pieces[(m, h)].bitcast(F32)
            t = ring.tile([P, 4, P], F32, name="gvp", tag="ring")
            for s in range(2):
                for u in range(2):
                    nc.tensor.transpose(t[:, 2 * s + u, :], words[:, s, u::2], ident[:])
            if h == 0:
                grp[m] = work.tile([P, 512, 4], BF16, name="grp", tag="grp", bufs=4, align_bytes=64)
            flat = grp[m][:].rearrange("p c t -> p (c t)").bitcast(F32)
            if m % 2 == 0:
                dst = flat.rearrange("p (u h r f) -> p h u r f", u=2, h=2, f=4)[:, h]
                src = t[:].rearrange("p f (r u) -> p u r f", u=2)
            else:
                dst = flat.rearrange("p (h s q u) -> p h s q u", h=2, s=2, u=2)[:, h]
                src = t[:].rearrange("p (s u) q -> p s q u", u=2)
            psum_copy(dst, src)

        def quant_tiles(tag, bufs):
            codes = work.tile([P, 512], U32, name=tag + "c", tag=tag + "c", bufs=bufs, align_bytes=64)
            scales = work.tile([P, 512], U8, name=tag + "s", tag=tag + "s", bufs=bufs, align_bytes=64)
            return codes, scales

        def quant(src, kind, pair, lo, hi):
            codes, scales = pair
            busy("v", 30 + 0.2235 * 4 * (hi - lo))
            nc.vector.quantize_mx(
                out=codes[:, lo:hi].bitcast(kind),
                scales=scales[:, lo:hi],
                in_=src[:, lo:hi, :].rearrange("p c t -> p (c t)"),
            )

        def quant_gv(m):
            gvc[m] = quant_tiles("gv", 7)
            quant(grp[m], E4M3X4 if m % 2 == 0 else E5M2X4, gvc[m], 0, 512)

        def quant_q(n):
            qqc[n] = quant_tiles("qq", 6)
            quant(gqx[n], E5M2X4, qqc[n], 0, 512)

        def quant_t(n):
            qtc[n] = quant_tiles("qt", 6)
            quant(gtx[n], E5M2X4, qtc[n], 0, 512)

        def inter_kq(which, b):
            t = work.tile([P, 2, D, 4], BF16, name="kqg", tag="kqg", bufs=2, align_bytes=64)
            kqg[(which, b)] = t
            busy("v", 30 + 522)
            nc.vector.tensor_copy(out=t[:], in_=kq_raw[(which, b)][:].rearrange("p c j d -> p c d j"))

        def quant_kq(which, b):
            codes = work.tile([P, 2, D], U32, name="kqc", tag="kqc", bufs=5, align_bytes=64)
            scales = work.tile([P, 2, D], U8, name="kqs", tag="kqs", bufs=5, align_bytes=64)
            busy("v", 30 + 229)
            nc.vector.quantize_mx(
                out=codes[:].rearrange("p c d -> p (c d)").bitcast(E4M3X4),
                scales=scales[:].rearrange("p c d -> p (c d)"),
                in_=kqg[(which, b)][:].rearrange("p c d j -> p (c d j)"),
            )
            kqc[(which, b)] = (codes, scales)

        def dp_unit(n, t):
            b, r = divmod(n, 4)
            g, c = divmod(r, 2)
            vc, vs = gvc[4 * b + 2 * c]
            gc, gs = gvc[4 * b + 2 * g + 1]
            o = ring.tile([P, 512], F32, name="dpb", tag="ring")
            cols = slice(P * t, P * (t + 1))
            nc.tensor.matmul_mx(
                out=o[:],
                lhsT=gc[:, cols].bitcast(E5M2X4),
                lhsT_scale=gs[:, cols],
                rhs=vc[:].bitcast(E4M3X4),
                rhs_scale=vs[:],
                start=True,
                stop=True,
            )
            if t == 0:
                dsx[n] = work.tile([P, 4, 512], BF16, name="ds", tag="ds", align_bytes=64)
            if load["s"] <= load["v"]:
                busy("s", 500)
                nc.scalar.activation(out=dsx[n][:, t, :], in_=o[:], func=COPY, scale=recip[:, 0:1])
            else:
                busy("v", 467)
                nc.vector.tensor_scalar(
                    out=dsx[n][:, t, :], in0=o[:], scalar1=recip[:, 0:1], scalar2=None, op0=MULT
                )

        def dst_unit(n, h):
            words = dsx[n][:].bitcast(F32)
            t = ring.tile([P, 4, P], F32, name="dst", tag="ring")
            for s in range(2):
                for u in range(2):
                    nc.tensor.transpose(t[:, 2 * s + u, :], words[:, 2 * h + s, P * u : P * (u + 1)], ident[:])
            if h == 0:
                gtx[n] = work.tile([P, 512, 4], BF16, name="gt", tag="gt", align_bytes=64)
            flat = gtx[n][:].rearrange("p c t -> p (c t)").bitcast(F32)
            psum_copy(
                flat.rearrange("p (q h f) -> p h q f", h=2, f=4)[:, h], t[:].rearrange("p f q -> p q f")
            )

        def inter_ds(n):
            gqx[n] = work.tile([P, 512, 4], BF16, name="gq", tag="gq", align_bytes=64)
            for u in range(2):
                busy("v", 531)
                nc.vector.tensor_copy(
                    out=gqx[n][:].rearrange("p (q u e) t -> p u q t e", u=2, e=2)[:, u],
                    in_=dsx[n][:].rearrange("p t (u q e) -> p u q t e", u=2, e=2)[:, u],
                )

        def mm_out(o, i, late):
            which, b, x = o
            if i == 0:
                if late:
                    acc[o] = ring.tile([P, 512], F32, name="late", tag="ring")
                else:
                    acc[o] = accp.tile([P, 512], F32, name="acc", tag="acc")
            sc, ss = kqc[(which, b)]
            mc, ms = qtc[4 * b + 2 * x + i] if which == 0 else qqc[4 * b + 2 * i + x]
            nc.tensor.matmul_mx(
                out=acc[o][:],
                lhsT=sc[:, i, :].bitcast(E4M3X4),
                lhsT_scale=ss[:, i, :],
                rhs=mc[:].bitcast(E5M2X4),
                rhs_scale=ms[:],
                start=(i == 0),
                stop=(i == 1),
            )

        def out_rows(o):
            which, b, x = o
            return (out_1 if which else out_0)[b, 512 * x : 512 * (x + 1), :]

        def out_copy(o, eng=None):
            which, b, x = o
            ot[o] = work.tile([P, 4, P], F32, name="ot", tag="ot", bufs=4)
            src = acc[o][:]
            psum_copy(ot[o][:], src.rearrange("p (q t) -> p t q", t=4), eng)

        def out_turn(o):
            t = ring.tile([P, 4, P], F32, name="turn", tag="ring")
            for j in range(4):
                nc.tensor.transpose(t[:, j, :], ot[o][:, j, :], ident[:])
            bank[o] = t

        def out_store(o, eng=None):
            rows = work.tile([P, 4, D], F32, name="rows", tag="rows", bufs=4)
            psum_copy(rows[:], bank[o][:], eng)
            nc.sync.dma_start(out=out_rows(o).rearrange("(p t) d -> p t d", t=4), in_=rows[:])

        def out_blocks(o):
            rows = work.tile([P, 16, 32], F32, name="blocks", tag="blocks", bufs=2, align_bytes=64)
            busy("v", 457)
            nc.vector.transpose(out=rows[:].rearrange("p b j -> p (b j)"), in_=acc[o][:])
            for a in range(4):
                lanes = slice(32 * a, 32 * (a + 1))
                nc.sync.dma_start(
                    out=out_rows(o)[:, lanes].rearrange("(b i) j -> i b j", i=32), in_=rows[lanes, :, :]
                )

        zeros = const.tile([P, 512], BF16, name="zeros")
        nc.gpsimd.memset(zeros[:], 0.0)

        def keep_clock(times):
            spin = accp.tile([P, 512], F32, name="acc", tag="acc")
            for i in range(times):
                nc.tensor.matmul(out=spin[:], lhsT=zeros[:, :P], rhs=zeros[:], start=True, stop=True)

        nc.vector.memset(warm[:], 1.0)
        nc.scalar.activation(out=warm[:], in_=warm[:], func=COPY, scale=1.0)
        keep_clock(7)
        gv_unit(0, 0)
        gv_unit(0, 1)
        nc.vector.reciprocal(out=recip[:], in_=div[:])
        gv_unit(1, 0)
        quant_gv(0)
        gvc[1] = quant_tiles("gv", 7)
        quant(grp[1], E5M2X4, gvc[1], 0, 256)
        gv_unit(1, 1)
        quant(grp[1], E5M2X4, gvc[1], 256, 512)
        gv_unit(2, 0)
        dp_unit(0, 0)
        dp_unit(0, 1)
        gv_unit(2, 1)
        dp_unit(0, 2)
        dp_unit(0, 3)
        quant_gv(2)
        inter_ds(0)
        gv_unit(3, 0)
        gv_unit(3, 1)

        out_at = {}
        for b in range(B):
            out_at[4 * b + 3] = (0, b, 0)
            out_at[4 * b + 4] = (1, b, 0)
            out_at[4 * b + 5] = (1, b, 1)
            out_at[4 * b + 6] = (0, b, 1)

        kq_at = {1: (0, 0), 2: (1, 0)}
        for b in range(1, B):
            kq_at[4 * b - 1] = (0, b)
            kq_at[4 * b] = (1, b)

        for n in range(1, STEPS):
            o = out_at.get(n)
            if n > 1:
                quant_t(n - 2)
            dp_unit(n, 0)
            dp_unit(n, 1)
            if o:
                mm_out(o, 0, False)
            if n > 1:
                inter_ds(n - 1)
            dst_unit(n - 1, 0)
            if n + 2 < STEPS:
                quant_gv(n + 2)
            if n - 1 in kq_at:
                which, kb = kq_at[n - 1]
                quant_kq(which, kb)
            if n + 3 < STEPS:
                gv_unit(n + 3, 0)
            quant_q(n - 1)
            dp_unit(n, 2)
            dp_unit(n, 3)
            if o:
                mm_out(o, 1, False)
                if n < STEPS - 1:
                    out_blocks(o)
                else:
                    out_copy(o)
            dst_unit(n - 1, 1)
            if n + 3 < STEPS:
                gv_unit(n + 3, 1)
            if n in kq_at:
                which, kb = kq_at[n]
                inter_kq(which, kb)

        n = STEPS
        o0, o1, o2, o3 = (0, B - 1, 0), (1, B - 1, 0), (0, B - 1, 1), (1, B - 1, 1)
        inter_ds(n - 1)
        dst_unit(n - 1, 0)
        dst_unit(n - 1, 1)
        mm_out(o1, 0, True)
        mm_out(o1, 1, True)
        quant_t(n - 2)
        out_turn(o0)
        keep_clock(2)
        out_copy(o1, "s")
        out_store(o0, "s")
        quant_t(n - 1)
        mm_out(o2, 0, True)
        mm_out(o3, 0, True)
        keep_clock(1)
        mm_out(o2, 1, True)
        quant_q(n - 1)
        mm_out(o3, 1, True)
        keep_clock(1)
        out_copy(o2, "s")
        out_copy(o3, "v")
        out_turn(o1)
        out_turn(o2)
        out_turn(o3)
        out_store(o1, "v")
        out_store(o2, "s")
        out_store(o3, "v")
